import numpy as np
import ml_dtypes


def mxq(x, axis, fmt="e4m3"):
    dtype, down = {"e4m3": (ml_dtypes.float8_e4m3fn, 7), "e5m2": (ml_dtypes.float8_e5m2, 14)}[fmt]
    v = np.moveaxis(np.asarray(x, np.float32).astype(ml_dtypes.bfloat16).astype(np.float64), axis, -1)
    blocks = v.reshape(v.shape[:-1] + (-1, 32))
    amax = np.abs(blocks).max(-1, keepdims=True)
    byte = np.maximum(np.where(amax > 0, np.frexp(amax)[1] - 1 + 127, 0) - down, 1)
    scale = np.exp2(byte - 127.0)
    codes = (blocks / scale).astype(np.float32).astype(dtype).astype(np.float64)
    return np.moveaxis((codes * scale).reshape(v.shape), -1, axis)


WIDE = False


def mx_kscale(k):
    if not WIDE:
        return np.ones(k)
    levels = np.array([20, -20, 10, -10, 0])
    a = np.random.permutation(np.resize(levels, k // 512 * 4)).reshape(k // 512, 4)
    idx = np.arange(k)
    return np.exp2(a[idx // 512, idx % 128 // 32])


BF16 = ml_dtypes.bfloat16


def bf(x):
    return np.asarray(x, np.float32).astype(BF16)


def f64(x):
    return np.asarray(x).astype(np.float64)


B, D, H = 1024, 512, 1024


def sigmoid(v):
    return 1.0 / (1.0 + np.exp(-v))


def setup_inputs():
    s = mx_kscale(B)[:, None]
    x0 = bf(np.random.standard_normal((B, D)))
    W_ih0 = bf(np.random.standard_normal((4 * H, D)) * 1.5 / np.sqrt(D))
    b_ih0 = bf(np.random.standard_normal(4 * H) * 0.3)
    b_hh0 = bf(np.random.standard_normal(4 * H) * 0.3)
    g = bf(np.random.standard_normal((B, H)) * np.exp2(np.random.randint(-12, 1, (B, 1))) * 4.0 / s)
    w = f64(W_ih0)
    b = f64(b_ih0) + f64(b_hh0)
    xf = f64(x0)
    a_i = xf @ w[:H].T + b[:H]
    a_g = xf @ w[2 * H:3 * H].T + b[2 * H:3 * H]
    a_o = xf @ w[3 * H:].T + b[3 * H:]
    return {"x": bf(f64(x0) * s), "W_ih0": W_ih0, "b_ih0": b_ih0, "b_hh0": b_hh0,
            "a_i": np.asarray(a_i, np.float32), "a_g": np.asarray(a_g, np.float32),
            "a_o": np.asarray(a_o, np.float32), "grad_out": g}


def reference(x, W_ih0, b_ih0, b_hh0, a_i, a_g, a_o, grad_out):
    go = f64(grad_out)
    gi = sigmoid(f64(a_i))
    gg = np.tanh(f64(a_g))
    gate_o = sigmoid(f64(a_o))
    tc = np.tanh(gi * gg)
    dc = go * gate_o * (1.0 - tc * tc)
    da_i = dc * gg * gi * (1.0 - gi)
    da_g = dc * gi * (1.0 - gg * gg)
    da_o = go * tc * gate_o * (1.0 - gate_o)
    da = np.concatenate([da_i, da_g, da_o], axis=1)
    dw = mxq(da, 0, "e5m2").T @ mxq(f64(x), 0, "e4m3")
    return np.concatenate([dw[:H], np.zeros((H, D)), dw[H:]], axis=0)

@@ -1,0 +1,202 @@
+from contextlib import ExitStack
+
+import concourse.mybir as mybir
+
+F32 = mybir.dt.float32
+BF16 = mybir.dt.bfloat16
+U32 = mybir.dt.uint32
+U8 = mybir.dt.uint8
+E4M3_X4 = mybir.dt.float8_e4m3fn_x4
+E5M2_X4 = mybir.dt.float8_e5m2_x4
+ACT = mybir.ActivationFunctionType
+ALU = mybir.AluOpType
+
+B, D, H = 1024, 512, 1024
+P = 128
+PACK = 4
+K_PASS = P * PACK
+PASSES = B // K_PASS
+COLS = 256
+BLOCKS = H // COLS
+ROUNDS = BLOCKS * PASSES
+M_TILE = 128
+M_TILES = COLS // M_TILE
+RUN = 4
+AHEAD = 2
+GATES = ("o", "i", "g")
+GATE_ROW = {"i": 0, "g": 2 * H, "o": 3 * H}
+ZERO_ROWS = H // P
+
+FLOPS = 2 * 3 * H * D * B
+BYTES = 2 * B * D + 3 * 4 * B * H + 2 * B * H + 4 * 4 * H * D
+
+
+def token_rows(dram, n, cols):
+    return dram[n * K_PASS : (n + 1) * K_PASS, cols].rearrange("(p j) w -> p j w", j=PACK)
+
+
+def by_rows(tile):
+    return tile[:].rearrange("p j (r i) -> p r j i", i=RUN)
+
+
+def by_words(tile):
+    return tile[:].rearrange("p (r i) j -> p r j i", i=RUN)
+
+
+def tile_lstmbaseline_pa_v_kernel(tc, x, W_ih0, b_ih0, b_hh0, a_i, a_g, a_o, grad_out, out):
+    nc = tc.nc
+    with ExitStack() as ctx:
+        ctx.enter_context(tc.manual_schedule())
+        const = ctx.enter_context(tc.tile_pool(name="const", bufs=1))
+        loads = ctx.enter_context(tc.tile_pool(name="loads", bufs=2))
+        work = ctx.enter_context(tc.tile_pool(name="work", bufs=2))
+        results = ctx.enter_context(tc.tile_pool(name="results", bufs=6))
+        psum = ctx.enter_context(tc.psum_pool(name="psum", bufs=1))
+
+        shape = [P, PACK, COLS]
+        saved = {}
+        gate = {}
+        cell = {}
+        codes = {}
+        scales = {}
+        acc = {}
+
+        zeros = const.tile([P, ZERO_ROWS * D], F32)
+        nc.vector.memset(zeros[:], 0.0)
+
+        x_raw = const.tile([P, PASSES, PACK, D], BF16)
+        x_words = const.tile([P, PASSES, D, PACK], BF16, align_bytes=64)
+        x_codes = const.tile([P, PASSES, D], U32, align_bytes=64)
+        x_scales = const.tile([P, PASSES, D], U8, align_bytes=64)
+
+        def load(k):
+            block, n = divmod(k, PASSES)
+            cols = slice(block * COLS, (block + 1) * COLS)
+            a_i_t = loads.tile(shape, F32, name="a_i_t")
+            a_g_t = loads.tile(shape, F32, name="a_g_t")
+            a_o_t = loads.tile(shape, F32, name="a_o_t")
+            go_t = loads.tile(shape, BF16, name="go_t", bufs=3)
+            nc.sync.dma_start(out=a_i_t[:], in_=token_rows(a_i, n, cols))
+            nc.sync.dma_start(out=a_g_t[:], in_=token_rows(a_g, n, cols))
+            nc.sync.dma_start(out=a_o_t[:], in_=token_rows(a_o, n, cols))
+            nc.sync.dma_start(out=go_t[:], in_=token_rows(grad_out, n, cols))
+            saved[k] = {"a_i": a_i_t, "a_g": a_g_t, "a_o": a_o_t, "go": go_t}
+
+        def gates(k):
+            i_t = work.tile(shape, F32, name="i_t")
+            g_t = work.tile(shape, F32, name="g_t")
+            o_t = work.tile(shape, F32, name="o_t")
+            gg_t = work.tile(shape, F32, name="gg_t")
+            nc.scalar.activation(out=i_t[:], in_=saved[k]["a_i"][:], func=ACT.Sigmoid)
+            nc.scalar.activation(out=g_t[:], in_=saved[k]["a_g"][:], func=ACT.Tanh)
+            nc.scalar.activation(out=o_t[:], in_=saved[k]["a_o"][:], func=ACT.Sigmoid)
+            nc.scalar.activation(out=gg_t[:], in_=g_t[:], func=ACT.Square)
+            gate[k] = {"i": i_t, "g": g_t, "o": o_t, "gg": gg_t}
+
+        def cell_state(k):
+            c_t = work.tile(shape, F32, name="c_t")
+            nc.vector.tensor_tensor(out=c_t[:], in0=gate[k]["i"][:], in1=gate[k]["g"][:], op=ALU.mult)
+            cell[k] = c_t
+
+        def quantise(k, name, da):
+            n = k % PASSES
+            nc.vector.quantize_mx(
+                out=codes[name][:, n, :].bitcast(E5M2_X4),
+                scales=scales[name][:, n, :],
+                in_=da[:].rearrange("p w j -> p (w j)"),
+            )
+
+        load(0)
+        load(1)
+        for n in range(PASSES):
+            nc.sync.dma_start(out=x_raw[:, n], in_=token_rows(x, n, slice(0, D)))
+        gates(0)
+        cell_state(0)
+
+        def drain(block):
+            for name in GATES:
+                for m in range(M_TILES):
+                    rows_t = results.tile([P, D], F32, name="rows_t")
+                    nc.scalar.copy(out=rows_t[:], in_=acc[name, m][:])
+                    row = GATE_ROW[name] + block * COLS + m * M_TILE
+                    nc.sync.dma_start(out=out[row : row + M_TILE, :], in_=rows_t[:])
+
+        for k in range(ROUNDS):
+            block, n = divmod(k, PASSES)
+
+            if k + AHEAD < ROUNDS:
+                load(k + AHEAD)
+            elif k + AHEAD == ROUNDS:
+                nc.sync.dma_start(
+                    out=out[H : 2 * H, :].rearrange("(p r) d -> p (r d)", p=P), in_=zeros[:]
+                )
+
+            ntc_t = work.tile(shape, F32, name="ntc_t")
+            tt_t = work.tile(shape, F32, name="tt_t")
+            nc.scalar.activation(out=ntc_t[:], in_=cell[k][:], func=ACT.Tanh, scale=-1.0)
+            nc.scalar.activation(out=tt_t[:], in_=ntc_t[:], func=ACT.Square)
+            if n == 0 and block > 0:
+                drain(block - 1)
+            if k + 1 < ROUNDS:
+                gates(k + 1)
+            if k < PASSES:
+                nc.scalar.copy(out=by_words(x_words[:, k]), in_=by_rows(x_raw[:, k]))
+
+            i_t, o_t, gg_t = gate[k]["i"], gate[k]["o"], gate[k]["gg"]
+            c_t, go_t = cell[k], saved[k]["go"]
+            if n == 0:
+                for name in GATES:
+                    codes[name] = work.tile([P, PASSES, COLS], U32, name="codes_" + name, align_bytes=64)
+                    scales[name] = work.tile([P, PASSES, COLS], U8, name="scales_" + name, align_bytes=64)
+            u_t = work.tile(shape, F32, name="u_t")
+            r_t = work.tile(shape, F32, name="r_t")
+            t_t = work.tile(shape, F32, name="t_t")
+            z_t = work.tile(shape, F32, name="z_t")
+            ndc_t = work.tile(shape, F32, name="ndc_t")
+            da_o = work.tile([P, COLS, PACK], BF16, name="da_o", align_bytes=64)
+            da_i = work.tile([P, COLS, PACK], BF16, name="da_i", align_bytes=64)
+            da_g = work.tile([P, COLS, PACK], BF16, name="da_g", align_bytes=64)
+            nc.vector.tensor_tensor(out=u_t[:], in0=o_t[:], in1=go_t[:], op=ALU.mult)
+            nc.vector.scalar_tensor_tensor(
+                out=r_t[:], in0=gg_t[:], scalar=1.0, in1=i_t[:], op0=ALU.subtract, op1=ALU.mult
+            )
+            nc.vector.scalar_tensor_tensor(
+                out=t_t[:], in0=o_t[:], scalar=1.0, in1=u_t[:], op0=ALU.subtract, op1=ALU.mult
+            )
+            nc.vector.scalar_tensor_tensor(
+                out=z_t[:], in0=i_t[:], scalar=1.0, in1=c_t[:], op0=ALU.subtract, op1=ALU.mult
+            )
+            nc.vector.tensor_tensor(out=by_words(da_o), in0=by_rows(ntc_t), in1=by_rows(t_t), op=ALU.mult)
+            nc.vector.scalar_tensor_tensor(
+                out=ndc_t[:], in0=tt_t[:], scalar=1.0, in1=u_t[:], op0=ALU.subtract, op1=ALU.mult
+            )
+            quantise(k, "o", da_o)
+            nc.vector.tensor_tensor(out=by_words(da_i), in0=by_rows(ndc_t), in1=by_rows(z_t), op=ALU.mult)
+            nc.vector.tensor_tensor(out=by_words(da_g), in0=by_rows(ndc_t), in1=by_rows(r_t), op=ALU.mult)
+            quantise(k, "i", da_i)
+            if k + 1 < ROUNDS:
+                cell_state(k + 1)
+            quantise(k, "g", da_g)
+            if k < PASSES:
+                nc.vector.quantize_mx(
+                    out=x_codes[:, k, :].bitcast(E4M3_X4),
+                    scales=x_scales[:, k, :],
+                    in_=x_words[:, k].rearrange("p d j -> p (d j)"),
+                )
+
+            for name in GATES:
+                for m in range(M_TILES):
+                    if n == 0:
+                        acc[name, m] = psum.tile([P, D], F32, name="acc_%s_%d" % (name, m))
+                    m_cols = slice(m * M_TILE, (m + 1) * M_TILE)
+                    nc.tensor.matmul_mx(
+                        out=acc[name, m][:],
+                        lhsT=codes[name][:, n, m_cols].bitcast(E5M2_X4),
+                        lhsT_scale=scales[name][:, n, m_cols],
+                        rhs=x_codes[:, n, :].bitcast(E4M3_X4),
+                        rhs_scale=x_scales[:, n, :],
+                        start=(n == 0),
+                        stop=(n == PASSES - 1),
+                    )
+
+        drain(BLOCKS - 1)

@@ -46,7 +46,6 @@ def by_words(tile):
 def tile_lstmbaseline_pa_v_kernel(tc, x, W_ih0, b_ih0, b_hh0, a_i, a_g, a_o, grad_out, out):
     nc = tc.nc
     with ExitStack() as ctx:
-        ctx.enter_context(tc.manual_schedule())
         const = ctx.enter_context(tc.tile_pool(name="const", bufs=1))
         loads = ctx.enter_context(tc.tile_pool(name="loads", bufs=2))
         work = ctx.enter_context(tc.tile_pool(name="work", bufs=2))

@@ -1,6 +1,7 @@
 from contextlib import ExitStack
 
 import concourse.mybir as mybir
+from concourse.masks import make_identity
 
 F32 = mybir.dt.float32
 BF16 = mybir.dt.bfloat16
@@ -23,7 +24,7 @@ M_TILE = 128
 M_TILES = COLS // M_TILE
 RUN = 4
 AHEAD = 2
-GATES = ("o", "i", "g")
+GATES = ("i", "o", "g")
 GATE_ROW = {"i": 0, "g": 2 * H, "o": 3 * H}
 ZERO_ROWS = H // P
 
@@ -43,22 +44,35 @@ def by_words(tile):
     return tile[:].rearrange("p (r i) j -> p r j i", i=RUN)
 
 
+def unit_cols(m):
+    return slice(m * M_TILE, (m + 1) * M_TILE)
+
+
 def tile_lstmbaseline_pa_v_kernel(tc, x, W_ih0, b_ih0, b_hh0, a_i, a_g, a_o, grad_out, out):
     nc = tc.nc
     with ExitStack() as ctx:
         const = ctx.enter_context(tc.tile_pool(name="const", bufs=1))
         loads = ctx.enter_context(tc.tile_pool(name="loads", bufs=2))
         work = ctx.enter_context(tc.tile_pool(name="work", bufs=2))
-        results = ctx.enter_context(tc.tile_pool(name="results", bufs=6))
-        psum = ctx.enter_context(tc.psum_pool(name="psum", bufs=1))
+        results = ctx.enter_context(tc.tile_pool(name="results", bufs=4))
+        psum = ctx.enter_context(tc.psum_pool(name="psum", bufs=2))
+        ctx.enter_context(tc.manual_schedule())
 
         shape = [P, PACK, COLS]
+        unit = [P, PACK, M_TILE]
         saved = {}
+        turned = {}
+        turned_gate = {}
+        gate_ps = {}
         gate = {}
-        cell = {}
+        made = {}
         codes = {}
         scales = {}
-        acc = {}
+        waiting = []
+        open_jobs = []
+
+        ident = const.tile([P, P], F32)
+        make_identity(nc, ident[:])
 
         zeros = const.tile([P, ZERO_ROWS * D], F32)
         nc.vector.memset(zeros[:], 0.0)
@@ -72,56 +86,153 @@ def tile_lstmbaseline_pa_v_kernel(tc, x, W_ih0, b_ih0, b_hh0, a_i, a_g, a_o, gra
             block, n = divmod(k, PASSES)
             cols = slice(block * COLS, (block + 1) * COLS)
             a_i_t = loads.tile(shape, F32, name="a_i_t")
-            a_g_t = loads.tile(shape, F32, name="a_g_t")
             a_o_t = loads.tile(shape, F32, name="a_o_t")
+            a_g_t = loads.tile(shape, F32, name="a_g_t")
             go_t = loads.tile(shape, BF16, name="go_t", bufs=3)
             nc.sync.dma_start(out=a_i_t[:], in_=token_rows(a_i, n, cols))
             nc.sync.dma_start(out=a_g_t[:], in_=token_rows(a_g, n, cols))
             nc.sync.dma_start(out=a_o_t[:], in_=token_rows(a_o, n, cols))
             nc.sync.dma_start(out=go_t[:], in_=token_rows(grad_out, n, cols))
-            saved[k] = {"a_i": a_i_t, "a_g": a_g_t, "a_o": a_o_t, "go": go_t}
+            saved[k] = {"i": a_i_t, "g": a_g_t, "o": a_o_t, "go": go_t}
 
-        def gates(k):
-            i_t = work.tile(shape, F32, name="i_t")
+        def turn(k, name, m):
+            a_ps = psum.tile(unit, F32, name="a_ps")
+            for j in range(PACK):
+                nc.tensor.transpose(a_ps[:, j, :], saved[k][name][:, j, unit_cols(m)], ident[:])
+            turned[k, name, m] = a_ps
+
+        def sigmoid(k, name, m):
+            s_t = work.tile(unit, F32, name="s_t", bufs=4)
+            nc.scalar.activation(out=s_t[:], in_=turned[k, name, m][:], func=ACT.Sigmoid)
+            turned_gate[k, name, m] = s_t
+
+        def turn_back(k, name, m):
+            s_ps = psum.tile(unit, F32, name="s_ps", bufs=4)
+            for j in range(PACK):
+                nc.tensor.transpose(s_ps[:, j, :], turned_gate[k, name, m][:, j, :], ident[:])
+            gate_ps[k, name, m] = s_ps
+
+        def cell_gate_tanh(k):
             g_t = work.tile(shape, F32, name="g_t")
-            o_t = work.tile(shape, F32, name="o_t")
+            nc.scalar.activation(out=g_t[:], in_=saved[k]["g"][:], func=ACT.Tanh)
+            gate[k] = {"g": g_t}
+
+        def cell_gate_square(k):
             gg_t = work.tile(shape, F32, name="gg_t")
-            nc.scalar.activation(out=i_t[:], in_=saved[k]["a_i"][:], func=ACT.Sigmoid)
-            nc.scalar.activation(out=g_t[:], in_=saved[k]["a_g"][:], func=ACT.Tanh)
-            nc.scalar.activation(out=o_t[:], in_=saved[k]["a_o"][:], func=ACT.Sigmoid)
-            nc.scalar.activation(out=gg_t[:], in_=g_t[:], func=ACT.Square)
-            gate[k] = {"i": i_t, "g": g_t, "o": o_t, "gg": gg_t}
+            nc.scalar.activation(out=gg_t[:], in_=gate[k]["g"][:], func=ACT.Square)
+            gate[k]["gg"] = gg_t
 
-        def cell_state(k):
-            c_t = work.tile(shape, F32, name="c_t")
-            nc.vector.tensor_tensor(out=c_t[:], in0=gate[k]["i"][:], in1=gate[k]["g"][:], op=ALU.mult)
-            cell[k] = c_t
-
-        def quantise(k, name, da):
-            n = k % PASSES
-            nc.vector.quantize_mx(
-                out=codes[name][:, n, :].bitcast(E5M2_X4),
-                scales=scales[name][:, n, :],
-                in_=da[:].rearrange("p w j -> p (w j)"),
+        def multiply(job, acc, n):
+            block, name, m = job
+            nc.tensor.matmul_mx(
+                out=acc[:],
+                lhsT=codes[block, name][:, n, unit_cols(m)].bitcast(E5M2_X4),
+                lhsT_scale=scales[block, name][:, n, unit_cols(m)],
+                rhs=x_codes[:, n, :].bitcast(E4M3_X4),
+                rhs_scale=x_scales[:, n, :],
+                start=(n == 0),
+                stop=(n == PASSES - 1),
             )
 
-        load(0)
-        load(1)
-        for n in range(PASSES):
-            nc.sync.dma_start(out=x_raw[:, n], in_=token_rows(x, n, slice(0, D)))
-        gates(0)
-        cell_state(0)
+        def store(job, acc, on_vector):
+            block, name, m = job
+            rows_t = results.tile([P, D], F32, name="rows_t")
+            if on_vector:
+                nc.vector.tensor_copy(out=rows_t[:], in_=acc[:])
+            else:
+                nc.scalar.copy(out=rows_t[:], in_=acc[:])
+            row = GATE_ROW[name] + block * COLS + m * M_TILE
+            nc.sync.dma_start(out=out[row : row + M_TILE, :], in_=rows_t[:])
 
-        def drain(block):
-            for name in GATES:
-                for m in range(M_TILES):
-                    rows_t = results.tile([P, D], F32, name="rows_t")
-                    nc.scalar.copy(out=rows_t[:], in_=acc[name, m][:])
-                    row = GATE_ROW[name] + block * COLS + m * M_TILE
-                    nc.sync.dma_start(out=out[row : row + M_TILE, :], in_=rows_t[:])
+        def product(k, name, m, in0, in1, minus_one):
+            dst = made[k][name][:, :, unit_cols(m)]
+            if minus_one:
+                nc.vector.scalar_tensor_tensor(
+                    out=dst, in0=in0, scalar=1.0, in1=in1, op0=ALU.subtract, op1=ALU.mult
+                )
+            else:
+                nc.vector.tensor_tensor(out=dst, in0=in0, in1=in1, op=ALU.mult)
 
-        for k in range(ROUNDS):
+        def part(tile, m):
+            return tile[:, :, unit_cols(m)]
+
+        ms = range(M_TILES)
+
+        def cell_state(k):
+            made[k] = {"c": work.tile(shape, F32, name="c_t")}
+            for m in ms:
+                product(k, "c", m, gate_ps[k, "i", m][:], part(gate[k]["g"], m), False)
+
+        def input_products(k):
+            made[k]["r"] = work.tile(shape, F32, name="r_t")
+            made[k]["z"] = work.tile(shape, F32, name="z_t")
+            for m in ms:
+                product(k, "r", m, part(gate[k]["gg"], m), gate_ps[k, "i", m][:], True)
+            for m in ms:
+                product(k, "z", m, gate_ps[k, "i", m][:], part(made[k]["c"], m), True)
+
+        def output_products(k):
+            made[k]["u"] = work.tile(shape, F32, name="u_t")
+            made[k]["t"] = work.tile(shape, F32, name="t_t")
+            for m in ms:
+                product(k, "u", m, gate_ps[k, "o", m][:], part(saved[k]["go"], m), False)
+            for m in ms:
+                product(k, "t", m, gate_ps[k, "o", m][:], part(made[k]["u"], m), True)
+
+        def cell_tanh(k):
+            ntc_t = work.tile(shape, F32, name="ntc_t")
+            tt_t = work.tile(shape, F32, name="tt_t")
+            nc.scalar.activation(out=ntc_t[:], in_=made[k]["c"][:], func=ACT.Tanh, scale=-1.0)
+            nc.scalar.activation(out=tt_t[:], in_=ntc_t[:], func=ACT.Square)
+            made[k]["ntc"] = ntc_t
+            made[k]["tt"] = tt_t
+
+        def cell_gradient(k):
+            ndc_t = work.tile(shape, F32, name="ndc_t")
+            nc.vector.scalar_tensor_tensor(
+                out=ndc_t[:], in0=made[k]["tt"][:], scalar=1.0, in1=made[k]["u"][:], op0=ALU.subtract, op1=ALU.mult
+            )
+            made[k]["ndc"] = ndc_t
+
+        def last_product(engine, k, name, a, b):
+            da = work.tile([P, COLS, PACK], BF16, name="da_" + name, align_bytes=64)
+            engine.tensor_tensor(out=by_words(da), in0=by_rows(made[k][a]), in1=by_rows(made[k][b]), op=ALU.mult)
+            made[k]["da_" + name] = da
+
+        def quantise(k, name):
             block, n = divmod(k, PASSES)
+            if n == 0:
+                codes[block, name] = work.tile([P, PASSES, COLS], U32, name="codes_" + name, align_bytes=64)
+                scales[block, name] = work.tile([P, PASSES, COLS], U8, name="scales_" + name, align_bytes=64)
+            nc.vector.quantize_mx(
+                out=codes[block, name][:, n, :].bitcast(E5M2_X4),
+                scales=scales[block, name][:, n, :],
+                in_=made[k]["da_" + name][:].rearrange("p w j -> p (w j)"),
+            )
+
+        filled = []
+
+        def fill_one():
+            if waiting:
+                job = waiting[0]
+                waiting.remove(job)
+                acc = psum.tile([P, D], F32, name="acc")
+                for n in range(PASSES):
+                    multiply(job, acc, n)
+                filled.append((job, acc))
+
+        def empty_one():
+            if filled:
+                pair = filled[0]
+                filled.remove(pair)
+                store(pair[0], pair[1], False)
+
+        load(0)
+        for k in range(-1, ROUNDS + 1):
+            after = k + 1
+            live = 0 <= k < ROUNDS
+            more = after < ROUNDS
+            last = k == ROUNDS
 
             if k + AHEAD < ROUNDS:
                 load(k + AHEAD)
@@ -129,73 +240,84 @@ def tile_lstmbaseline_pa_v_kernel(tc, x, W_ih0, b_ih0, b_hh0, a_i, a_g, a_o, gra
                 nc.sync.dma_start(
                     out=out[H : 2 * H, :].rearrange("(p r) d -> p (r d)", p=P), in_=zeros[:]
                 )
+            if k == -1:
+                for n in range(PASSES):
+                    nc.sync.dma_start(out=x_raw[:, n], in_=token_rows(x, n, slice(0, D)))
 
-            ntc_t = work.tile(shape, F32, name="ntc_t")
-            tt_t = work.tile(shape, F32, name="tt_t")
-            nc.scalar.activation(out=ntc_t[:], in_=cell[k][:], func=ACT.Tanh, scale=-1.0)
-            nc.scalar.activation(out=tt_t[:], in_=ntc_t[:], func=ACT.Square)
-            if n == 0 and block > 0:
-                drain(block - 1)
-            if k + 1 < ROUNDS:
-                gates(k + 1)
-            if k < PASSES:
+            if more:
+                for m in ms:
+                    turn(after, "i", m)
+                for m in ms:
+                    sigmoid(after, "i", m)
+                cell_gate_tanh(after)
+                for m in ms:
+                    turn(after, "o", m)
+            fill_one()
+            if k > 0:
+                cell_gradient(k - 1)
+                helper = nc.vector if last else nc.gpsimd
+                last_product(helper, k - 1, "i", "ndc", "z")
+                last_product(helper, k - 1, "o", "ntc", "t")
+                if last:
+                    quantise(k - 1, "i")
+                    for m in ms:
+                        multiply(open_jobs[m][0], open_jobs[m][1], PASSES - 1)
+            if live:
+                input_products(k)
+            if more:
+                for m in ms:
+                    turn_back(after, "i", m)
+            fill_one()
+            if live:
+                cell_tanh(k)
+            empty_one()
+            if live:
+                output_products(k)
+            if more:
+                for m in ms:
+                    sigmoid(after, "o", m)
+            empty_one()
+            if more:
+                for m in ms:
+                    turn_back(after, "o", m)
+            fill_one()
+            if more:
+                cell_state(after)
+                cell_gate_square(after)
+            empty_one()
+            if not more:
+                for q in range(len(waiting)):
+                    fill_one()
+                    empty_one()
+            if 0 <= k < PASSES:
                 nc.scalar.copy(out=by_words(x_words[:, k]), in_=by_rows(x_raw[:, k]))
-
-            i_t, o_t, gg_t = gate[k]["i"], gate[k]["o"], gate[k]["gg"]
-            c_t, go_t = cell[k], saved[k]["go"]
-            if n == 0:
+            if k > 0:
+                last_product(nc.vector, k - 1, "g", "ndc", "r")
                 for name in GATES:
-                    codes[name] = work.tile([P, PASSES, COLS], U32, name="codes_" + name, align_bytes=64)
-                    scales[name] = work.tile([P, PASSES, COLS], U8, name="scales_" + name, align_bytes=64)
-            u_t = work.tile(shape, F32, name="u_t")
-            r_t = work.tile(shape, F32, name="r_t")
-            t_t = work.tile(shape, F32, name="t_t")
-            z_t = work.tile(shape, F32, name="z_t")
-            ndc_t = work.tile(shape, F32, name="ndc_t")
-            da_o = work.tile([P, COLS, PACK], BF16, name="da_o", align_bytes=64)
-            da_i = work.tile([P, COLS, PACK], BF16, name="da_i", align_bytes=64)
-            da_g = work.tile([P, COLS, PACK], BF16, name="da_g", align_bytes=64)
-            nc.vector.tensor_tensor(out=u_t[:], in0=o_t[:], in1=go_t[:], op=ALU.mult)
-            nc.vector.scalar_tensor_tensor(
-                out=r_t[:], in0=gg_t[:], scalar=1.0, in1=i_t[:], op0=ALU.subtract, op1=ALU.mult
-            )
-            nc.vector.scalar_tensor_tensor(
-                out=t_t[:], in0=o_t[:], scalar=1.0, in1=u_t[:], op0=ALU.subtract, op1=ALU.mult
-            )
-            nc.vector.scalar_tensor_tensor(
-                out=z_t[:], in0=i_t[:], scalar=1.0, in1=c_t[:], op0=ALU.subtract, op1=ALU.mult
-            )
-            nc.vector.tensor_tensor(out=by_words(da_o), in0=by_rows(ntc_t), in1=by_rows(t_t), op=ALU.mult)
-            nc.vector.scalar_tensor_tensor(
-                out=ndc_t[:], in0=tt_t[:], scalar=1.0, in1=u_t[:], op0=ALU.subtract, op1=ALU.mult
-            )
-            quantise(k, "o", da_o)
-            nc.vector.tensor_tensor(out=by_words(da_i), in0=by_rows(ndc_t), in1=by_rows(z_t), op=ALU.mult)
-            nc.vector.tensor_tensor(out=by_words(da_g), in0=by_rows(ndc_t), in1=by_rows(r_t), op=ALU.mult)
-            quantise(k, "i", da_i)
-            if k + 1 < ROUNDS:
-                cell_state(k + 1)
-            quantise(k, "g", da_g)
-            if k < PASSES:
-                nc.vector.quantize_mx(
-                    out=x_codes[:, k, :].bitcast(E4M3_X4),
-                    scales=x_scales[:, k, :],
-                    in_=x_words[:, k].rearrange("p d j -> p (d j)"),
-                )
-
-            for name in GATES:
-                for m in range(M_TILES):
-                    if n == 0:
-                        acc[name, m] = psum.tile([P, D], F32, name="acc_%s_%d" % (name, m))
-                    m_cols = slice(m * M_TILE, (m + 1) * M_TILE)
-                    nc.tensor.matmul_mx(
-                        out=acc[name, m][:],
-                        lhsT=codes[name][:, n, m_cols].bitcast(E5M2_X4),
-                        lhsT_scale=scales[name][:, n, m_cols],
-                        rhs=x_codes[:, n, :].bitcast(E4M3_X4),
-                        rhs_scale=x_scales[:, n, :],
-                        start=(n == 0),
-                        stop=(n == PASSES - 1),
+                    if not (last and name == "i"):
+                        quantise(k - 1, name)
+                if k <= PASSES:
+                    nc.vector.quantize_mx(
+                        out=x_codes[:, k - 1, :].bitcast(E4M3_X4),
+                        scales=x_scales[:, k - 1, :],
+                        in_=x_words[:, k - 1].rearrange("p d j -> p (d j)"),
                     )
+                block, n = divmod(k - 1, PASSES)
+                jobs = [(block, name, m) for name in GATES for m in ms]
+                if block < BLOCKS - 1:
+                    if n == PASSES - 1:
+                        waiting.extend(jobs)
+                elif n == 0:
+                    for q, job in enumerate(jobs):
+                        if q < 4:
+                            bank = psum.tile([P, D], F32, name="s_ps", bufs=4)
+                        else:
+                            bank = psum.tile([P, D], F32, name="a_ps")
+                        multiply(job, bank, 0)
+                        open_jobs.append((job, bank))
 
-        drain(BLOCKS - 1)
+        for q, pair in enumerate(open_jobs):
+            if q >= M_TILES:
+                multiply(pair[0], pair[1], PASSES - 1)
+        for q, pair in enumerate(open_jobs):
+            store(pair[0], pair[1], q == len(open_jobs) - 1)

@@ -54,7 +54,7 @@ def tile_lstmbaseline_pa_v_kernel(tc, x, W_ih0, b_ih0, b_hh0, a_i, a_g, a_o, gra
         const = ctx.enter_context(tc.tile_pool(name="const", bufs=1))
         loads = ctx.enter_context(tc.tile_pool(name="loads", bufs=2))
         work = ctx.enter_context(tc.tile_pool(name="work", bufs=2))
-        results = ctx.enter_context(tc.tile_pool(name="results", bufs=4))
+        results = ctx.enter_context(tc.tile_pool(name="results", bufs=8))
         psum = ctx.enter_context(tc.psum_pool(name="psum", bufs=2))
         ctx.enter_context(tc.manual_schedule())
 
@@ -89,8 +89,14 @@ def tile_lstmbaseline_pa_v_kernel(tc, x, W_ih0, b_ih0, b_hh0, a_i, a_g, a_o, gra
             a_o_t = loads.tile(shape, F32, name="a_o_t")
             a_g_t = loads.tile(shape, F32, name="a_g_t")
             go_t = loads.tile(shape, BF16, name="go_t", bufs=3)
-            nc.sync.dma_start(out=a_i_t[:], in_=token_rows(a_i, n, cols))
-            nc.sync.dma_start(out=a_g_t[:], in_=token_rows(a_g, n, cols))
+            if k == 0:
+                for m in range(M_TILES):
+                    half = slice(m * M_TILE, (m + 1) * M_TILE)
+                    nc.sync.dma_start(out=a_i_t[:, :, half], in_=token_rows(a_i, n, half))
+                    nc.sync.dma_start(out=a_g_t[:, :, half], in_=token_rows(a_g, n, half))
+            else:
+                nc.sync.dma_start(out=a_i_t[:], in_=token_rows(a_i, n, cols))
+                nc.sync.dma_start(out=a_g_t[:], in_=token_rows(a_g, n, cols))
             nc.sync.dma_start(out=a_o_t[:], in_=token_rows(a_o, n, cols))
             nc.sync.dma_start(out=go_t[:], in_=token_rows(grad_out, n, cols))
             saved[k] = {"i": a_i_t, "g": a_g_t, "o": a_o_t, "go": go_t}
@@ -112,10 +118,10 @@ def tile_lstmbaseline_pa_v_kernel(tc, x, W_ih0, b_ih0, b_hh0, a_i, a_g, a_o, gra
                 nc.tensor.transpose(s_ps[:, j, :], turned_gate[k, name, m][:, j, :], ident[:])
             gate_ps[k, name, m] = s_ps
 
-        def cell_gate_tanh(k):
-            g_t = work.tile(shape, F32, name="g_t")
-            nc.scalar.activation(out=g_t[:], in_=saved[k]["g"][:], func=ACT.Tanh)
-            gate[k] = {"g": g_t}
+        def cell_gate_tanh(k, cols):
+            if k not in gate:
+                gate[k] = {"g": work.tile(shape, F32, name="g_t")}
+            nc.scalar.activation(out=gate[k]["g"][:, :, cols], in_=saved[k]["g"][:, :, cols], func=ACT.Tanh)
 
         def cell_gate_square(k):
             gg_t = work.tile(shape, F32, name="gg_t")
@@ -232,6 +238,7 @@ def tile_lstmbaseline_pa_v_kernel(tc, x, W_ih0, b_ih0, b_hh0, a_i, a_g, a_o, gra
             after = k + 1
             live = 0 <= k < ROUNDS
             more = after < ROUNDS
+            first = k == -1
             last = k == ROUNDS
 
             if k + AHEAD < ROUNDS:
@@ -245,13 +252,18 @@ def tile_lstmbaseline_pa_v_kernel(tc, x, W_ih0, b_ih0, b_hh0, a_i, a_g, a_o, gra
                     nc.sync.dma_start(out=x_raw[:, n], in_=token_rows(x, n, slice(0, D)))
 
             if more:
-                for m in ms:
-                    turn(after, "i", m)
-                for m in ms:
-                    sigmoid(after, "i", m)
-                cell_gate_tanh(after)
-                for m in ms:
-                    turn(after, "o", m)
+                if first:
+                    for m in ms:
+                        turn(after, "i", m)
+                    for m in ms:
+                        sigmoid(after, "i", m)
+                        cell_gate_tanh(after, unit_cols(m))
+                else:
+                    for m in ms:
+                        sigmoid(after, "i", m)
+                    cell_gate_tanh(after, slice(0, COLS))
+                    for m in ms:
+                        turn(after, "o", m)
             fill_one()
             if k > 0:
                 cell_gradient(k - 1)
@@ -259,31 +271,37 @@ def tile_lstmbaseline_pa_v_kernel(tc, x, W_ih0, b_ih0, b_hh0, a_i, a_g, a_o, gra
                 last_product(helper, k - 1, "i", "ndc", "z")
                 last_product(helper, k - 1, "o", "ntc", "t")
                 if last:
-                    quantise(k - 1, "i")
-                    for m in ms:
-                        multiply(open_jobs[m][0], open_jobs[m][1], PASSES - 1)
+                    for q, name in enumerate(("i", "o")):
+                        quantise(k - 1, name)
+                        for m in ms:
+                            multiply(open_jobs[q * M_TILES + m][0], open_jobs[q * M_TILES + m][1], PASSES - 1)
             if live:
                 input_products(k)
             if more:
                 for m in ms:
                     turn_back(after, "i", m)
+                if first:
+                    for m in ms:
+                        turn(after, "o", m)
             fill_one()
             if live:
                 cell_tanh(k)
             empty_one()
+            fill_one()
             if live:
                 output_products(k)
             if more:
+                cell_gate_square(after)
                 for m in ms:
                     sigmoid(after, "o", m)
+                if after + 1 < ROUNDS:
+                    for m in ms:
+                        turn(after + 1, "i", m)
             empty_one()
             if more:
                 for m in ms:
                     turn_back(after, "o", m)
-            fill_one()
-            if more:
                 cell_state(after)
-                cell_gate_square(after)
             empty_one()
             if not more:
                 for q in range(len(waiting)):
@@ -294,7 +312,7 @@ def tile_lstmbaseline_pa_v_kernel(tc, x, W_ih0, b_ih0, b_hh0, a_i, a_g, a_o, gra
             if k > 0:
                 last_product(nc.vector, k - 1, "g", "ndc", "r")
                 for name in GATES:
-                    if not (last and name == "i"):
+                    if not (last and name != "g"):
                         quantise(k - 1, name)
                 if k <= PASSES:
                     nc.vector.quantize_mx(
@@ -317,7 +335,7 @@ def tile_lstmbaseline_pa_v_kernel(tc, x, W_ih0, b_ih0, b_hh0, a_i, a_g, a_o, gra
                         open_jobs.append((job, bank))
 
         for q, pair in enumerate(open_jobs):
-            if q >= M_TILES:
+            if q >= 2 * M_TILES:
                 multiply(pair[0], pair[1], PASSES - 1)
         for q, pair in enumerate(open_jobs):
             store(pair[0], pair[1], q == len(open_jobs) - 1)

@@ -23,6 +23,7 @@ ROUNDS = BLOCKS * PASSES
 M_TILE = 128
 M_TILES = COLS // M_TILE
 RUN = 4
+HELPED = 64
 AHEAD = 2
 GATES = ("i", "o", "g")
 GATE_ROW = {"i": 0, "g": 2 * H, "o": 3 * H}
@@ -37,11 +38,11 @@ def token_rows(dram, n, cols):
 
 
 def by_rows(tile):
-    return tile[:].rearrange("p j (r i) -> p r j i", i=RUN)
+    return tile.rearrange("p j (r i) -> p r j i", i=RUN)
 
 
 def by_words(tile):
-    return tile[:].rearrange("p (r i) j -> p r j i", i=RUN)
+    return tile.rearrange("p (r i) j -> p r j i", i=RUN)
 
 
 def unit_cols(m):
@@ -130,10 +131,12 @@ def tile_lstmbaseline_pa_v_kernel(tc, x, W_ih0, b_ih0, b_hh0, a_i, a_g, a_o, gra
 
         def multiply(job, acc, n):
             block, name, m = job
+            at = GATES.index(name) * COLS + m * M_TILE
+            these = slice(at, at + M_TILE)
             nc.tensor.matmul_mx(
                 out=acc[:],
-                lhsT=codes[block, name][:, n, unit_cols(m)].bitcast(E5M2_X4),
-                lhsT_scale=scales[block, name][:, n, unit_cols(m)],
+                lhsT=codes[block][:, n, these].bitcast(E5M2_X4),
+                lhsT_scale=scales[block][:, n, these],
                 rhs=x_codes[:, n, :].bitcast(E4M3_X4),
                 rhs_scale=x_scales[:, n, :],
                 start=(n == 0),
@@ -171,7 +174,9 @@ def tile_lstmbaseline_pa_v_kernel(tc, x, W_ih0, b_ih0, b_hh0, a_i, a_g, a_o, gra
 
         def input_products(k):
             made[k]["r"] = work.tile(shape, F32, name="r_t")
-            made[k]["z"] = work.tile(shape, F32, name="z_t")
+            made[k]["zt"] = work.tile([P, PACK, 2 * COLS], F32, name="zt_t")
+            made[k]["z"] = made[k]["zt"][:, :, 0:COLS]
+            made[k]["t"] = made[k]["zt"][:, :, COLS : 2 * COLS]
             for m in ms:
                 product(k, "r", m, part(gate[k]["gg"], m), gate_ps[k, "i", m][:], True)
             for m in ms:
@@ -179,41 +184,55 @@ def tile_lstmbaseline_pa_v_kernel(tc, x, W_ih0, b_ih0, b_hh0, a_i, a_g, a_o, gra
 
         def output_products(k):
             made[k]["u"] = work.tile(shape, F32, name="u_t")
-            made[k]["t"] = work.tile(shape, F32, name="t_t")
             for m in ms:
                 product(k, "u", m, gate_ps[k, "o", m][:], part(saved[k]["go"], m), False)
             for m in ms:
                 product(k, "t", m, gate_ps[k, "o", m][:], part(made[k]["u"], m), True)
 
         def cell_tanh(k):
-            ntc_t = work.tile(shape, F32, name="ntc_t")
+            made[k]["dt"] = work.tile([P, PACK, 2 * COLS], F32, name="dt_t")
+            made[k]["ndc"] = made[k]["dt"][:, :, 0:COLS]
+            made[k]["ntc"] = made[k]["dt"][:, :, COLS : 2 * COLS]
             tt_t = work.tile(shape, F32, name="tt_t")
-            nc.scalar.activation(out=ntc_t[:], in_=made[k]["c"][:], func=ACT.Tanh, scale=-1.0)
-            nc.scalar.activation(out=tt_t[:], in_=ntc_t[:], func=ACT.Square)
-            made[k]["ntc"] = ntc_t
+            nc.scalar.activation(out=made[k]["ntc"], in_=made[k]["c"][:], func=ACT.Tanh, scale=-1.0)
+            nc.scalar.activation(out=tt_t[:], in_=made[k]["ntc"], func=ACT.Square)
             made[k]["tt"] = tt_t
 
         def cell_gradient(k):
-            ndc_t = work.tile(shape, F32, name="ndc_t")
             nc.vector.scalar_tensor_tensor(
-                out=ndc_t[:], in0=made[k]["tt"][:], scalar=1.0, in1=made[k]["u"][:], op0=ALU.subtract, op1=ALU.mult
+                out=made[k]["ndc"], in0=made[k]["tt"][:], scalar=1.0, in1=made[k]["u"][:], op0=ALU.subtract, op1=ALU.mult
             )
-            made[k]["ndc"] = ndc_t
 
-        def last_product(engine, k, name, a, b):
-            da = work.tile([P, COLS, PACK], BF16, name="da_" + name, align_bytes=64)
-            engine.tensor_tensor(out=by_words(da), in0=by_rows(made[k][a]), in1=by_rows(made[k][b]), op=ALU.mult)
-            made[k]["da_" + name] = da
+        def last_product(engine, k, name, a, b, cols=slice(0, COLS)):
+            if "da" not in made[k]:
+                made[k]["da"] = work.tile([P, len(GATES) * COLS, PACK], BF16, name="da_t", align_bytes=64)
+            at = GATES.index(name) * COLS
+            engine.tensor_tensor(
+                out=by_words(made[k]["da"][:, at + cols.start : at + cols.stop, :]),
+                in0=by_rows(made[k][a][:, :, cols]),
+                in1=by_rows(made[k][b][:, :, cols]),
+                op=ALU.mult,
+            )
 
-        def quantise(k, name):
+        def two_last_products(k):
+            made[k]["da"] = work.tile([P, len(GATES) * COLS, PACK], BF16, name="da_t", align_bytes=64)
+            nc.gpsimd.tensor_tensor(
+                out=by_words(made[k]["da"][:, 0 : 2 * COLS, :]),
+                in0=by_rows(made[k]["dt"][:]),
+                in1=by_rows(made[k]["zt"][:]),
+                op=ALU.mult,
+            )
+
+        def quantise(k, first_gate, gates):
             block, n = divmod(k, PASSES)
-            if n == 0:
-                codes[block, name] = work.tile([P, PASSES, COLS], U32, name="codes_" + name, align_bytes=64)
-                scales[block, name] = work.tile([P, PASSES, COLS], U8, name="scales_" + name, align_bytes=64)
+            if block not in codes:
+                codes[block] = work.tile([P, PASSES, len(GATES) * COLS], U32, name="codes_t", align_bytes=64)
+                scales[block] = work.tile([P, PASSES, len(GATES) * COLS], U8, name="scales_t", align_bytes=64)
+            these = slice(first_gate * COLS, (first_gate + gates) * COLS)
             nc.vector.quantize_mx(
-                out=codes[block, name][:, n, :].bitcast(E5M2_X4),
-                scales=scales[block, name][:, n, :],
-                in_=made[k]["da_" + name][:].rearrange("p w j -> p (w j)"),
+                out=codes[block][:, n, these].bitcast(E5M2_X4),
+                scales=scales[block][:, n, these],
+                in_=made[k]["da"][:, these, :].rearrange("p w j -> p (w j)"),
             )
 
         filled = []
@@ -267,14 +286,16 @@ def tile_lstmbaseline_pa_v_kernel(tc, x, W_ih0, b_ih0, b_hh0, a_i, a_g, a_o, gra
             fill_one()
             if k > 0:
                 cell_gradient(k - 1)
-                helper = nc.vector if last else nc.gpsimd
-                last_product(helper, k - 1, "i", "ndc", "z")
-                last_product(helper, k - 1, "o", "ntc", "t")
                 if last:
-                    for q, name in enumerate(("i", "o")):
-                        quantise(k - 1, name)
-                        for m in ms:
-                            multiply(open_jobs[q * M_TILES + m][0], open_jobs[q * M_TILES + m][1], PASSES - 1)
+                    last_product(nc.vector, k - 1, "i", "ndc", "z")
+                    last_product(nc.vector, k - 1, "o", "ntc", "t")
+                else:
+                    two_last_products(k - 1)
+                    last_product(nc.gpsimd, k - 1, "g", "ndc", "r", slice(0, HELPED))
+                if last:
+                    quantise(k - 1, 0, 2)
+                    for q in range(2 * M_TILES):
+                        multiply(open_jobs[q][0], open_jobs[q][1], PASSES - 1)
             if live:
                 input_products(k)
             if more:
@@ -310,10 +331,10 @@ def tile_lstmbaseline_pa_v_kernel(tc, x, W_ih0, b_ih0, b_hh0, a_i, a_g, a_o, gra
             if 0 <= k < PASSES:
                 nc.scalar.copy(out=by_words(x_words[:, k]), in_=by_rows(x_raw[:, k]))
             if k > 0:
-                last_product(nc.vector, k - 1, "g", "ndc", "r")
-                for name in GATES:
-                    if not (last and name != "g"):
-                        quantise(k - 1, name)
+                last_product(nc.vector, k - 1, "g", "ndc", "r", slice(0 if last else HELPED, COLS))
+                if not last:
+                    quantise(k - 1, 0, 2)
+                quantise(k - 1, 2, 1)
                 if k <= PASSES:
                     nc.vector.quantize_mx(
                         out=x_codes[:, k - 1, :].bitcast(E4M3_X4),

@@ -65,6 +65,7 @@ def tile_lstmbaseline_pa_v_kernel(tc, x, W_ih0, b_ih0, b_hh0, a_i, a_g, a_o, gra
         turned = {}
         turned_gate = {}
         gate_ps = {}
+        trio = {}
         gate = {}
         made = {}
         codes = {}
@@ -119,15 +120,25 @@ def tile_lstmbaseline_pa_v_kernel(tc, x, W_ih0, b_ih0, b_hh0, a_i, a_g, a_o, gra
                 nc.tensor.transpose(s_ps[:, j, :], turned_gate[k, name, m][:, j, :], ident[:])
             gate_ps[k, name, m] = s_ps
 
+        def trio_of(k):
+            if k not in trio:
+                trio[k] = work.tile([P, PACK, 3 * COLS], F32, name="trio_t")
+            return trio[k]
+
         def cell_gate_tanh(k, cols):
             if k not in gate:
-                gate[k] = {"g": work.tile(shape, F32, name="g_t")}
+                gate[k] = {"g": trio_of(k - 1)[:, :, 2 * COLS : 3 * COLS]}
             nc.scalar.activation(out=gate[k]["g"][:, :, cols], in_=saved[k]["g"][:, :, cols], func=ACT.Tanh)
 
-        def cell_gate_square(k):
-            gg_t = work.tile(shape, F32, name="gg_t")
-            nc.scalar.activation(out=gg_t[:], in_=gate[k]["g"][:], func=ACT.Square)
-            gate[k]["gg"] = gg_t
+        def squares(k):
+            lo = COLS if 0 <= k else 2 * COLS
+            hi = 3 * COLS if k + 1 < ROUNDS else 2 * COLS
+            sq_t = work.tile([P, PACK, 2 * COLS], F32, name="sq_t")
+            nc.scalar.activation(out=sq_t[:, :, lo - COLS : hi - COLS], in_=trio[k][:, :, lo:hi], func=ACT.Square)
+            if 0 <= k:
+                made[k]["tt"] = sq_t[:, :, 0:COLS]
+            if k + 1 < ROUNDS:
+                gate[k + 1]["gg"] = sq_t[:, :, COLS : 2 * COLS]
 
         def multiply(job, acc, n):
             block, name, m = job
@@ -190,17 +201,14 @@ def tile_lstmbaseline_pa_v_kernel(tc, x, W_ih0, b_ih0, b_hh0, a_i, a_g, a_o, gra
                 product(k, "t", m, gate_ps[k, "o", m][:], part(made[k]["u"], m), True)
 
         def cell_tanh(k):
-            made[k]["dt"] = work.tile([P, PACK, 2 * COLS], F32, name="dt_t")
-            made[k]["ndc"] = made[k]["dt"][:, :, 0:COLS]
-            made[k]["ntc"] = made[k]["dt"][:, :, COLS : 2 * COLS]
-            tt_t = work.tile(shape, F32, name="tt_t")
+            made[k]["dt"] = trio_of(k)[:, :, 0 : 2 * COLS]
+            made[k]["ndc"] = trio_of(k)[:, :, 0:COLS]
+            made[k]["ntc"] = trio_of(k)[:, :, COLS : 2 * COLS]
             nc.scalar.activation(out=made[k]["ntc"], in_=made[k]["c"][:], func=ACT.Tanh, scale=-1.0)
-            nc.scalar.activation(out=tt_t[:], in_=made[k]["ntc"], func=ACT.Square)
-            made[k]["tt"] = tt_t
 
         def cell_gradient(k):
             nc.vector.scalar_tensor_tensor(
-                out=made[k]["ndc"], in0=made[k]["tt"][:], scalar=1.0, in1=made[k]["u"][:], op0=ALU.subtract, op1=ALU.mult
+                out=made[k]["ndc"], in0=made[k]["tt"], scalar=1.0, in1=made[k]["u"][:], op0=ALU.subtract, op1=ALU.mult
             )
 
         def last_product(engine, k, name, a, b, cols=slice(0, COLS)):
@@ -218,7 +226,7 @@ def tile_lstmbaseline_pa_v_kernel(tc, x, W_ih0, b_ih0, b_hh0, a_i, a_g, a_o, gra
             made[k]["da"] = work.tile([P, len(GATES) * COLS, PACK], BF16, name="da_t", align_bytes=64)
             nc.gpsimd.tensor_tensor(
                 out=by_words(made[k]["da"][:, 0 : 2 * COLS, :]),
-                in0=by_rows(made[k]["dt"][:]),
+                in0=by_rows(made[k]["dt"]),
                 in1=by_rows(made[k]["zt"][:]),
                 op=ALU.mult,
             )
@@ -237,11 +245,11 @@ def tile_lstmbaseline_pa_v_kernel(tc, x, W_ih0, b_ih0, b_hh0, a_i, a_g, a_o, gra
 
         filled = []
 
-        def fill_one():
+        def fill_one(bank_of="acc"):
             if waiting:
                 job = waiting[0]
                 waiting.remove(job)
-                acc = psum.tile([P, D], F32, name="acc")
+                acc = psum.tile([P, D], F32, name=bank_of)
                 for n in range(PASSES):
                     multiply(job, acc, n)
                 filled.append((job, acc))
@@ -284,6 +292,10 @@ def tile_lstmbaseline_pa_v_kernel(tc, x, W_ih0, b_ih0, b_hh0, a_i, a_g, a_o, gra
                     for m in ms:
                         turn(after, "o", m)
             fill_one()
+            if not more:
+                fill_one()
+                fill_one("a_ps")
+                fill_one("a_ps")
             if k > 0:
                 cell_gradient(k - 1)
                 if last:
@@ -304,15 +316,20 @@ def tile_lstmbaseline_pa_v_kernel(tc, x, W_ih0, b_ih0, b_hh0, a_i, a_g, a_o, gra
                 if first:
                     for m in ms:
                         turn(after, "o", m)
+            if not more:
+                empty_one()
+                empty_one()
+                fill_one()
             fill_one()
             if live:
                 cell_tanh(k)
+            if live or more:
+                squares(k)
             empty_one()
             fill_one()
             if live:
                 output_products(k)
             if more:
-                cell_gate_square(after)
                 for m in ms:
                     sigmoid(after, "o", m)
                 if after + 1 < ROUNDS:

@@ -22,7 +22,7 @@ BLOCKS = H // COLS
 ROUNDS = BLOCKS * PASSES
 M_TILE = 128
 M_TILES = COLS // M_TILE
-RUN = 4
+RUN = 8
 HELPED = 64
 AHEAD = 2
 GATES = ("i", "o", "g")

@@ -25,6 +25,7 @@ M_TILES = COLS // M_TILE
 RUN = 8
 HELPED = 64
 AHEAD = 2
+EARLY = 2
 GATES = ("i", "o", "g")
 GATE_ROW = {"i": 0, "g": 2 * H, "o": 3 * H}
 ZERO_ROWS = H // P
@@ -134,7 +135,9 @@ def tile_lstmbaseline_pa_v_kernel(tc, x, W_ih0, b_ih0, b_hh0, a_i, a_g, a_o, gra
             lo = COLS if 0 <= k else 2 * COLS
             hi = 3 * COLS if k + 1 < ROUNDS else 2 * COLS
             sq_t = work.tile([P, PACK, 2 * COLS], F32, name="sq_t")
-            nc.scalar.activation(out=sq_t[:, :, lo - COLS : hi - COLS], in_=trio[k][:, :, lo:hi], func=ACT.Square)
+            cuts = [lo, 2 * COLS, hi] if k == 0 else [lo, hi]
+            for a, b in zip(cuts[:-1], cuts[1:]):
+                nc.scalar.activation(out=sq_t[:, :, a - COLS : b - COLS], in_=trio[k][:, :, a:b], func=ACT.Square)
             if 0 <= k:
                 made[k]["tt"] = sq_t[:, :, 0:COLS]
             if k + 1 < ROUNDS:
@@ -178,18 +181,27 @@ def tile_lstmbaseline_pa_v_kernel(tc, x, W_ih0, b_ih0, b_hh0, a_i, a_g, a_o, gra
 
         ms = range(M_TILES)
 
-        def cell_state(k):
-            made[k] = {"c": work.tile(shape, F32, name="c_t")}
-            for m in ms:
-                product(k, "c", m, gate_ps[k, "i", m][:], part(gate[k]["g"], m), False)
-
-        def input_products(k):
-            made[k]["r"] = work.tile(shape, F32, name="r_t")
+        def pair_tile(k):
             made[k]["zt"] = work.tile([P, PACK, 2 * COLS], F32, name="zt_t")
             made[k]["z"] = made[k]["zt"][:, :, 0:COLS]
             made[k]["t"] = made[k]["zt"][:, :, COLS : 2 * COLS]
+
+        def cell_state(k):
+            made[k] = {"c": work.tile(shape, F32, name="c_t")}
+            if k == 0:
+                pair_tile(k)
+            for m in ms:
+                product(k, "c", m, gate_ps[k, "i", m][:], part(gate[k]["g"], m), False)
+                if k == 0:
+                    product(k, "z", m, gate_ps[k, "i", m][:], part(made[k]["c"], m), True)
+
+        def input_products(k):
+            made[k]["r"] = work.tile(shape, F32, name="r_t")
             for m in ms:
                 product(k, "r", m, part(gate[k]["gg"], m), gate_ps[k, "i", m][:], True)
+            if k == 0:
+                return
+            pair_tile(k)
             for m in ms:
                 product(k, "z", m, gate_ps[k, "i", m][:], part(made[k]["c"], m), True)
 
@@ -231,12 +243,14 @@ def tile_lstmbaseline_pa_v_kernel(tc, x, W_ih0, b_ih0, b_hh0, a_i, a_g, a_o, gra
                 op=ALU.mult,
             )
 
-        def quantise(k, first_gate, gates):
+        def quantise(k, first_gate, gates, half=None):
             block, n = divmod(k, PASSES)
             if block not in codes:
                 codes[block] = work.tile([P, PASSES, len(GATES) * COLS], U32, name="codes_t", align_bytes=64)
                 scales[block] = work.tile([P, PASSES, len(GATES) * COLS], U8, name="scales_t", align_bytes=64)
             these = slice(first_gate * COLS, (first_gate + gates) * COLS)
+            if half is not None:
+                these = slice(first_gate * COLS + half * M_TILE, first_gate * COLS + (half + 1) * M_TILE)
             nc.vector.quantize_mx(
                 out=codes[block][:, n, these].bitcast(E5M2_X4),
                 scales=scales[block][:, n, these],
@@ -278,6 +292,8 @@ def tile_lstmbaseline_pa_v_kernel(tc, x, W_ih0, b_ih0, b_hh0, a_i, a_g, a_o, gra
                 for n in range(PASSES):
                     nc.sync.dma_start(out=x_raw[:, n], in_=token_rows(x, n, slice(0, D)))
 
+            if k == 0:
+                cell_tanh(k)
             if more:
                 if first:
                     for m in ms:
@@ -289,39 +305,34 @@ def tile_lstmbaseline_pa_v_kernel(tc, x, W_ih0, b_ih0, b_hh0, a_i, a_g, a_o, gra
                     for m in ms:
                         sigmoid(after, "i", m)
                     cell_gate_tanh(after, slice(0, COLS))
-                    for m in ms:
-                        turn(after, "o", m)
             fill_one()
             if not more:
                 fill_one()
                 fill_one("a_ps")
                 fill_one("a_ps")
+            if last:
+                last_product(nc.vector, k - 1, "o", "ntc", "t")
             if k > 0:
                 cell_gradient(k - 1)
-                if last:
-                    last_product(nc.vector, k - 1, "i", "ndc", "z")
-                    last_product(nc.vector, k - 1, "o", "ntc", "t")
-                else:
+                if not last:
                     two_last_products(k - 1)
-                    last_product(nc.gpsimd, k - 1, "g", "ndc", "r", slice(0, HELPED))
-                if last:
-                    quantise(k - 1, 0, 2)
-                    for q in range(2 * M_TILES):
-                        multiply(open_jobs[q][0], open_jobs[q][1], PASSES - 1)
+                    if more:
+                        last_product(nc.gpsimd, k - 1, "g", "ndc", "r", slice(0, HELPED))
             if live:
                 input_products(k)
             if more:
                 for m in ms:
                     turn_back(after, "i", m)
+                for m in ms:
+                    turn(after, "o", m)
                 if first:
-                    for m in ms:
-                        turn(after, "o", m)
+                    cell_state(after)
             if not more:
                 empty_one()
                 empty_one()
                 fill_one()
             fill_one()
-            if live:
+            if live and k > 0:
                 cell_tanh(k)
             if live or more:
                 squares(k)
@@ -332,14 +343,19 @@ def tile_lstmbaseline_pa_v_kernel(tc, x, W_ih0, b_ih0, b_hh0, a_i, a_g, a_o, gra
             if more:
                 for m in ms:
                     sigmoid(after, "o", m)
+                if k < EARLY:
+                    for m in ms:
+                        turn_back(after, "o", m)
                 if after + 1 < ROUNDS:
                     for m in ms:
                         turn(after + 1, "i", m)
             empty_one()
             if more:
-                for m in ms:
-                    turn_back(after, "o", m)
-                cell_state(after)
+                if k >= EARLY:
+                    for m in ms:
+                        turn_back(after, "o", m)
+                if not first:
+                    cell_state(after)
             empty_one()
             if not more:
                 for q in range(len(waiting)):
@@ -347,11 +363,28 @@ def tile_lstmbaseline_pa_v_kernel(tc, x, W_ih0, b_ih0, b_hh0, a_i, a_g, a_o, gra
                     empty_one()
             if 0 <= k < PASSES:
                 nc.scalar.copy(out=by_words(x_words[:, k]), in_=by_rows(x_raw[:, k]))
-            if k > 0:
-                last_product(nc.vector, k - 1, "g", "ndc", "r", slice(0 if last else HELPED, COLS))
-                if not last:
-                    quantise(k - 1, 0, 2)
+            if last:
+                def close(first_job, jobs_closed):
+                    for q in range(first_job, first_job + jobs_closed):
+                        multiply(open_jobs[q][0], open_jobs[q][1], PASSES - 1)
+                        store(open_jobs[q][0], open_jobs[q][1], q == len(open_jobs) - 1)
+
+                quantise(k - 1, 1, 1)
+                close(M_TILES, M_TILES)
+                last_product(nc.vector, k - 1, "i", "ndc", "z")
+                last_product(nc.vector, k - 1, "g", "ndc", "r", unit_cols(0))
+                quantise(k - 1, 0, 1)
+                close(0, M_TILES)
+                last_product(nc.vector, k - 1, "g", "ndc", "r", unit_cols(1))
+                quantise(k - 1, 2, 1, 0)
+                close(2 * M_TILES, 1)
+                quantise(k - 1, 2, 1, 1)
+                close(2 * M_TILES + 1, 1)
+            elif k > 0:
+                last_product(nc.vector, k - 1, "g", "ndc", "r", slice(HELPED if more else 0, COLS))
+                quantise(k - 1, 0, 2)
                 quantise(k - 1, 2, 1)
+            if k > 0:
                 if k <= PASSES:
                     nc.vector.quantize_mx(
                         out=x_codes[:, k - 1, :].bitcast(E4M3_X4),
@@ -371,9 +404,3 @@ def tile_lstmbaseline_pa_v_kernel(tc, x, W_ih0, b_ih0, b_hh0, a_i, a_g, a_o, gra
                             bank = psum.tile([P, D], F32, name="a_ps")
                         multiply(job, bank, 0)
                         open_jobs.append((job, bank))
-
-        for q, pair in enumerate(open_jobs):
-            if q >= 2 * M_TILES:
-                multiply(pair[0], pair[1], PASSES - 1)
-        for q, pair in enumerate(open_jobs):
-            store(pair[0], pair[1], q == len(open_jobs) - 1)

@@ -24,7 +24,7 @@ M_TILE = 128
 M_TILES = COLS // M_TILE
 RUN = 8
 HELPED = 64
-AHEAD = 2
+AHEAD = 3
 EARLY = 2
 GATES = ("i", "o", "g")
 GATE_ROW = {"i": 0, "g": 2 * H, "o": 3 * H}
@@ -54,7 +54,7 @@ def tile_lstmbaseline_pa_v_kernel(tc, x, W_ih0, b_ih0, b_hh0, a_i, a_g, a_o, gra
     nc = tc.nc
     with ExitStack() as ctx:
         const = ctx.enter_context(tc.tile_pool(name="const", bufs=1))
-        loads = ctx.enter_context(tc.tile_pool(name="loads", bufs=2))
+        loads = ctx.enter_context(tc.tile_pool(name="loads", bufs=3))
         work = ctx.enter_context(tc.tile_pool(name="work", bufs=2))
         results = ctx.enter_context(tc.tile_pool(name="results", bufs=8))
         psum = ctx.enter_context(tc.psum_pool(name="psum", bufs=2))
@@ -91,7 +91,7 @@ def tile_lstmbaseline_pa_v_kernel(tc, x, W_ih0, b_ih0, b_hh0, a_i, a_g, a_o, gra
             a_i_t = loads.tile(shape, F32, name="a_i_t")
             a_o_t = loads.tile(shape, F32, name="a_o_t")
             a_g_t = loads.tile(shape, F32, name="a_g_t")
-            go_t = loads.tile(shape, BF16, name="go_t", bufs=3)
+            go_t = loads.tile(shape, BF16, name="go_t", bufs=4)
             if k == 0:
                 for m in range(M_TILES):
                     half = slice(m * M_TILE, (m + 1) * M_TILE)
@@ -275,6 +275,7 @@ def tile_lstmbaseline_pa_v_kernel(tc, x, W_ih0, b_ih0, b_hh0, a_i, a_g, a_o, gra
                 store(pair[0], pair[1], False)
 
         load(0)
+        load(1)
         for k in range(-1, ROUNDS + 1):
             after = k + 1
             live = 0 <= k < ROUNDS
@@ -282,15 +283,15 @@ def tile_lstmbaseline_pa_v_kernel(tc, x, W_ih0, b_ih0, b_hh0, a_i, a_g, a_o, gra
             first = k == -1
             last = k == ROUNDS
 
+            if k == -1:
+                for n in range(PASSES):
+                    nc.sync.dma_start(out=x_raw[:, n], in_=token_rows(x, n, slice(0, D)))
             if k + AHEAD < ROUNDS:
                 load(k + AHEAD)
             elif k + AHEAD == ROUNDS:
                 nc.sync.dma_start(
                     out=out[H : 2 * H, :].rearrange("(p r) d -> p (r d)", p=P), in_=zeros[:]
                 )
-            if k == -1:
-                for n in range(PASSES):
-                    nc.sync.dma_start(out=x_raw[:, n], in_=token_rows(x, n, slice(0, D)))
 
             if k == 0:
                 cell_tanh(k)

from contextlib import ExitStack

import concourse.mybir as mybir
from concourse.masks import make_identity

F32 = mybir.dt.float32
BF16 = mybir.dt.bfloat16
U32 = mybir.dt.uint32
U8 = mybir.dt.uint8
E4M3_X4 = mybir.dt.float8_e4m3fn_x4
E5M2_X4 = mybir.dt.float8_e5m2_x4
ACT = mybir.ActivationFunctionType
ALU = mybir.AluOpType

B, D, H = 1024, 512, 1024
P = 128
PACK = 4
K_PASS = P * PACK
PASSES = B // K_PASS
COLS = 256
BLOCKS = H // COLS
ROUNDS = BLOCKS * PASSES
M_TILE = 128
M_TILES = COLS // M_TILE
RUN = 8
HELPED = 64
AHEAD = 3
EARLY = 2
GATES = ("i", "o", "g")
GATE_ROW = {"i": 0, "g": 2 * H, "o": 3 * H}
ZERO_ROWS = H // P

FLOPS = 2 * 3 * H * D * B
BYTES = 2 * B * D + 3 * 4 * B * H + 2 * B * H + 4 * 4 * H * D


def token_rows(dram, n, cols):
    return dram[n * K_PASS : (n + 1) * K_PASS, cols].rearrange("(p j) w -> p j w", j=PACK)


def by_rows(tile):
    return tile.rearrange("p j (r i) -> p r j i", i=RUN)


def by_words(tile):
    return tile.rearrange("p (r i) j -> p r j i", i=RUN)


def unit_cols(m):
    return slice(m * M_TILE, (m + 1) * M_TILE)


def tile_lstmbaseline_pa_v_kernel(tc, x, W_ih0, b_ih0, b_hh0, a_i, a_g, a_o, grad_out, out):
    nc = tc.nc
    with ExitStack() as ctx:
        const = ctx.enter_context(tc.tile_pool(name="const", bufs=1))
        loads = ctx.enter_context(tc.tile_pool(name="loads", bufs=3))
        work = ctx.enter_context(tc.tile_pool(name="work", bufs=2))
        results = ctx.enter_context(tc.tile_pool(name="results", bufs=8))
        psum = ctx.enter_context(tc.psum_pool(name="psum", bufs=2))
        ctx.enter_context(tc.manual_schedule())

        shape = [P, PACK, COLS]
        unit = [P, PACK, M_TILE]
        saved = {}
        turned = {}
        turned_gate = {}
        gate_ps = {}
        trio = {}
        gate = {}
        made = {}
        codes = {}
        scales = {}
        waiting = []
        open_jobs = []

        ident = const.tile([P, P], F32)
        make_identity(nc, ident[:])

        zeros = const.tile([P, ZERO_ROWS * D], F32)
        nc.vector.memset(zeros[:], 0.0)

        x_raw = const.tile([P, PASSES, PACK, D], BF16)
        x_words = const.tile([P, PASSES, D, PACK], BF16, align_bytes=64)
        x_codes = const.tile([P, PASSES, D], U32, align_bytes=64)
        x_scales = const.tile([P, PASSES, D], U8, align_bytes=64)

        def load(k):
            block, n = divmod(k, PASSES)
            cols = slice(block * COLS, (block + 1) * COLS)
            a_i_t = loads.tile(shape, F32, name="a_i_t")
            a_o_t = loads.tile(shape, F32, name="a_o_t")
            a_g_t = loads.tile(shape, F32, name="a_g_t")
            go_t = loads.tile(shape, BF16, name="go_t", bufs=4)
            if k == 0:
                for m in range(M_TILES):
                    half = slice(m * M_TILE, (m + 1) * M_TILE)
                    nc.sync.dma_start(out=a_i_t[:, :, half], in_=token_rows(a_i, n, half))
                    nc.sync.dma_start(out=a_g_t[:, :, half], in_=token_rows(a_g, n, half))
            else:
                nc.sync.dma_start(out=a_i_t[:], in_=token_rows(a_i, n, cols))
                nc.sync.dma_start(out=a_g_t[:], in_=token_rows(a_g, n, cols))
            nc.sync.dma_start(out=a_o_t[:], in_=token_rows(a_o, n, cols))
            nc.sync.dma_start(out=go_t[:], in_=token_rows(grad_out, n, cols))
            saved[k] = {"i": a_i_t, "g": a_g_t, "o": a_o_t, "go": go_t}

        def turn(k, name, m):
            a_ps = psum.tile(unit, F32, name="a_ps")
            for j in range(PACK):
                nc.tensor.transpose(a_ps[:, j, :], saved[k][name][:, j, unit_cols(m)], ident[:])
            turned[k, name, m] = a_ps

        def sigmoid(k, name, m):
            s_t = work.tile(unit, F32, name="s_t", bufs=4)
            nc.scalar.activation(out=s_t[:], in_=turned[k, name, m][:], func=ACT.Sigmoid)
            turned_gate[k, name, m] = s_t

        def turn_back(k, name, m):
            s_ps = psum.tile(unit, F32, name="s_ps", bufs=4)
            for j in range(PACK):
                nc.tensor.transpose(s_ps[:, j, :], turned_gate[k, name, m][:, j, :], ident[:])
            gate_ps[k, name, m] = s_ps

        def trio_of(k):
            if k not in trio:
                trio[k] = work.tile([P, PACK, 3 * COLS], F32, name="trio_t")
            return trio[k]

        def cell_gate_tanh(k, cols):
            if k not in gate:
                gate[k] = {"g": trio_of(k - 1)[:, :, 2 * COLS : 3 * COLS]}
            nc.scalar.activation(out=gate[k]["g"][:, :, cols], in_=saved[k]["g"][:, :, cols], func=ACT.Tanh)

        def squares(k):
            lo = COLS if 0 <= k else 2 * COLS
            hi = 3 * COLS if k + 1 < ROUNDS else 2 * COLS
            sq_t = work.tile([P, PACK, 2 * COLS], F32, name="sq_t")
            cuts = [lo, 2 * COLS, hi] if k == 0 else [lo, hi]
            for a, b in zip(cuts[:-1], cuts[1:]):
                nc.scalar.activation(out=sq_t[:, :, a - COLS : b - COLS], in_=trio[k][:, :, a:b], func=ACT.Square)
            if 0 <= k:
                made[k]["tt"] = sq_t[:, :, 0:COLS]
            if k + 1 < ROUNDS:
                gate[k + 1]["gg"] = sq_t[:, :, COLS : 2 * COLS]

        def multiply(job, acc, n):
            block, name, m = job
            at = GATES.index(name) * COLS + m * M_TILE
            these = slice(at, at + M_TILE)
            nc.tensor.matmul_mx(
                out=acc[:],
                lhsT=codes[block][:, n, these].bitcast(E5M2_X4),
                lhsT_scale=scales[block][:, n, these],
                rhs=x_codes[:, n, :].bitcast(E4M3_X4),
                rhs_scale=x_scales[:, n, :],
                start=(n == 0),
                stop=(n == PASSES - 1),
            )

        def store(job, acc, on_vector):
            block, name, m = job
            rows_t = results.tile([P, D], F32, name="rows_t")
            if on_vector:
                nc.vector.tensor_copy(out=rows_t[:], in_=acc[:])
            else:
                nc.scalar.copy(out=rows_t[:], in_=acc[:])
            row = GATE_ROW[name] + block * COLS + m * M_TILE
            nc.sync.dma_start(out=out[row : row + M_TILE, :], in_=rows_t[:])

        def product(k, name, m, in0, in1, minus_one):
            dst = made[k][name][:, :, unit_cols(m)]
            if minus_one:
                nc.vector.scalar_tensor_tensor(
                    out=dst, in0=in0, scalar=1.0, in1=in1, op0=ALU.subtract, op1=ALU.mult
                )
            else:
                nc.vector.tensor_tensor(out=dst, in0=in0, in1=in1, op=ALU.mult)

        def part(tile, m):
            return tile[:, :, unit_cols(m)]

        ms = range(M_TILES)

        def pair_tile(k):
            made[k]["zt"] = work.tile([P, PACK, 2 * COLS], F32, name="zt_t")
            made[k]["z"] = made[k]["zt"][:, :, 0:COLS]
            made[k]["t"] = made[k]["zt"][:, :, COLS : 2 * COLS]

        def cell_state(k):
            made[k] = {"c": work.tile(shape, F32, name="c_t")}
            if k == 0:
                pair_tile(k)
            for m in ms:
                product(k, "c", m, gate_ps[k, "i", m][:], part(gate[k]["g"], m), False)
                if k == 0:
                    product(k, "z", m, gate_ps[k, "i", m][:], part(made[k]["c"], m), True)

        def input_products(k):
            made[k]["r"] = work.tile(shape, F32, name="r_t")
            for m in ms:
                product(k, "r", m, part(gate[k]["gg"], m), gate_ps[k, "i", m][:], True)
            if k == 0:
                return
            pair_tile(k)
            for m in ms:
                product(k, "z", m, gate_ps[k, "i", m][:], part(made[k]["c"], m), True)

        def output_products(k):
            made[k]["u"] = work.tile(shape, F32, name="u_t")
            for m in ms:
                product(k, "u", m, gate_ps[k, "o", m][:], part(saved[k]["go"], m), False)
            for m in ms:
                product(k, "t", m, gate_ps[k, "o", m][:], part(made[k]["u"], m), True)

        def cell_tanh(k):
            made[k]["dt"] = trio_of(k)[:, :, 0 : 2 * COLS]
            made[k]["ndc"] = trio_of(k)[:, :, 0:COLS]
            made[k]["ntc"] = trio_of(k)[:, :, COLS : 2 * COLS]
            nc.scalar.activation(out=made[k]["ntc"], in_=made[k]["c"][:], func=ACT.Tanh, scale=-1.0)

        def cell_gradient(k):
            nc.vector.scalar_tensor_tensor(
                out=made[k]["ndc"], in0=made[k]["tt"], scalar=1.0, in1=made[k]["u"][:], op0=ALU.subtract, op1=ALU.mult
            )

        def last_product(engine, k, name, a, b, cols=slice(0, COLS)):
            if "da" not in made[k]:
                made[k]["da"] = work.tile([P, len(GATES) * COLS, PACK], BF16, name="da_t", align_bytes=64)
            at = GATES.index(name) * COLS
            engine.tensor_tensor(
                out=by_words(made[k]["da"][:, at + cols.start : at + cols.stop, :]),
                in0=by_rows(made[k][a][:, :, cols]),
                in1=by_rows(made[k][b][:, :, cols]),
                op=ALU.mult,
            )

        def two_last_products(k):
            made[k]["da"] = work.tile([P, len(GATES) * COLS, PACK], BF16, name="da_t", align_bytes=64)
            nc.gpsimd.tensor_tensor(
                out=by_words(made[k]["da"][:, 0 : 2 * COLS, :]),
                in0=by_rows(made[k]["dt"]),
                in1=by_rows(made[k]["zt"][:]),
                op=ALU.mult,
            )

        def quantise(k, first_gate, gates, half=None):
            block, n = divmod(k, PASSES)
            if block not in codes:
                codes[block] = work.tile([P, PASSES, len(GATES) * COLS], U32, name="codes_t", align_bytes=64)
                scales[block] = work.tile([P, PASSES, len(GATES) * COLS], U8, name="scales_t", align_bytes=64)
            these = slice(first_gate * COLS, (first_gate + gates) * COLS)
            if half is not None:
                these = slice(first_gate * COLS + half * M_TILE, first_gate * COLS + (half + 1) * M_TILE)
            nc.vector.quantize_mx(
                out=codes[block][:, n, these].bitcast(E5M2_X4),
                scales=scales[block][:, n, these],
                in_=made[k]["da"][:, these, :].rearrange("p w j -> p (w j)"),
            )

        filled = []

        def fill_one(bank_of="acc"):
            if waiting:
                job = waiting[0]
                waiting.remove(job)
                acc = psum.tile([P, D], F32, name=bank_of)
                for n in range(PASSES):
                    multiply(job, acc, n)
                filled.append((job, acc))

        def empty_one():
            if filled:
                pair = filled[0]
                filled.remove(pair)
                store(pair[0], pair[1], False)

        load(0)
        load(1)
        for k in range(-1, ROUNDS + 1):
            after = k + 1
            live = 0 <= k < ROUNDS
            more = after < ROUNDS
            first = k == -1
            last = k == ROUNDS

            if k == -1:
                for n in range(PASSES):
                    nc.sync.dma_start(out=x_raw[:, n], in_=token_rows(x, n, slice(0, D)))
            if k + AHEAD < ROUNDS:
                load(k + AHEAD)
            elif k + AHEAD == ROUNDS:
                nc.sync.dma_start(
                    out=out[H : 2 * H, :].rearrange("(p r) d -> p (r d)", p=P), in_=zeros[:]
                )

            if k == 0:
                cell_tanh(k)
            if more:
                if first:
                    for m in ms:
                        turn(after, "i", m)
                    for m in ms:
                        sigmoid(after, "i", m)
                        cell_gate_tanh(after, unit_cols(m))
                else:
                    for m in ms:
                        sigmoid(after, "i", m)
                    cell_gate_tanh(after, slice(0, COLS))
            fill_one()
            if not more:
                fill_one()
                fill_one("a_ps")
                fill_one("a_ps")
            if last:
                last_product(nc.vector, k - 1, "o", "ntc", "t")
            if k > 0:
                cell_gradient(k - 1)
                if not last:
                    two_last_products(k - 1)
                    if more:
                        last_product(nc.gpsimd, k - 1, "g", "ndc", "r", slice(0, HELPED))
            if live:
                input_products(k)
            if more:
                for m in ms:
                    turn_back(after, "i", m)
                for m in ms:
                    turn(after, "o", m)
                if first:
                    cell_state(after)
            if not more:
                empty_one()
                empty_one()
                fill_one()
            fill_one()
            if live and k > 0:
                cell_tanh(k)
            if live or more:
                squares(k)
            empty_one()
            fill_one()
            if live:
                output_products(k)
            if more:
                for m in ms:
                    sigmoid(after, "o", m)
                if k < EARLY:
                    for m in ms:
                        turn_back(after, "o", m)
                if after + 1 < ROUNDS:
                    for m in ms:
                        turn(after + 1, "i", m)
            empty_one()
            if more:
                if k >= EARLY:
                    for m in ms:
                        turn_back(after, "o", m)
                if not first:
                    cell_state(after)
            empty_one()
            if not more:
                for q in range(len(waiting)):
                    fill_one()
                    empty_one()
            if 0 <= k < PASSES:
                nc.scalar.copy(out=by_words(x_words[:, k]), in_=by_rows(x_raw[:, k]))
            if last:
                def close(first_job, jobs_closed):
                    for q in range(first_job, first_job + jobs_closed):
                        multiply(open_jobs[q][0], open_jobs[q][1], PASSES - 1)
                        store(open_jobs[q][0], open_jobs[q][1], q == len(open_jobs) - 1)

                quantise(k - 1, 1, 1)
                close(M_TILES, M_TILES)
                last_product(nc.vector, k - 1, "i", "ndc", "z")
                last_product(nc.vector, k - 1, "g", "ndc", "r", unit_cols(0))
                quantise(k - 1, 0, 1)
                close(0, M_TILES)
                last_product(nc.vector, k - 1, "g", "ndc", "r", unit_cols(1))
                quantise(k - 1, 2, 1, 0)
                close(2 * M_TILES, 1)
                quantise(k - 1, 2, 1, 1)
                close(2 * M_TILES + 1, 1)
            elif k > 0:
                last_product(nc.vector, k - 1, "g", "ndc", "r", slice(HELPED if more else 0, COLS))
                quantise(k - 1, 0, 2)
                quantise(k - 1, 2, 1)
            if k > 0:
                if k <= PASSES:
                    nc.vector.quantize_mx(
                        out=x_codes[:, k - 1, :].bitcast(E4M3_X4),
                        scales=x_scales[:, k - 1, :],
                        in_=x_words[:, k - 1].rearrange("p d j -> p (d j)"),
                    )
                block, n = divmod(k - 1, PASSES)
                jobs = [(block, name, m) for name in GATES for m in ms]
                if block < BLOCKS - 1:
                    if n == PASSES - 1:
                        waiting.extend(jobs)
                elif n == 0:
                    for q, job in enumerate(jobs):
                        if q < 4:
                            bank = psum.tile([P, D], F32, name="s_ps", bufs=4)
                        else:
                            bank = psum.tile([P, D], F32, name="a_ps")
                        multiply(job, bank, 0)
                        open_jobs.append((job, bank))
